import numpy as np
import ml_dtypes


def mxq(x, axis, fmt="e4m3"):
    dtype, down = {"e4m3": (ml_dtypes.float8_e4m3fn, 7), "e5m2": (ml_dtypes.float8_e5m2, 14)}[fmt]
    v = np.moveaxis(np.asarray(x, np.float32).astype(ml_dtypes.bfloat16).astype(np.float64), axis, -1)
    blocks = v.reshape(v.shape[:-1] + (-1, 32))
    amax = np.abs(blocks).max(-1, keepdims=True)
    byte = np.maximum(np.where(amax > 0, np.frexp(amax)[1] - 1 + 127, 0) - down, 1)
    scale = np.exp2(byte - 127.0)
    codes = (blocks / scale).astype(np.float32).astype(dtype).astype(np.float64)
    return np.moveaxis((codes * scale).reshape(v.shape), -1, axis)


WIDE = False


def mx_kscale(k):
    if not WIDE:
        return np.ones(k)
    levels = np.array([30, -30])
    if k % 512:
        return np.exp2(np.random.permutation(np.resize(levels, k // 32))).repeat(32)
    a = np.empty((k // 512, 16))
    for p in range(k // 512):
        a[p, :8] = np.random.permutation(np.resize(levels, 8))
        for g in range(8):
            far = levels[np.abs(levels - a[p, g]) >= 10]
            a[p, g + 8] = far[np.random.randint(len(far))]
    return np.exp2(a.ravel()).repeat(32)


BF16 = ml_dtypes.bfloat16


def bf(x):
    return np.asarray(x, np.float32).astype(BF16)


def f64(x):
    return np.asarray(x).astype(np.float64)


E2M1 = np.array([0.0, 0.5, 1.0, 1.5, 2.0, 3.0, 4.0, 6.0, -0.0, -0.5, -1.0, -1.5, -2.0, -3.0, -4.0, -6.0])


def pack_weight(w, fmt):
    k, n = w.shape
    w = f64(bf(w)).reshape(k // 32, 32, n)
    amax = np.abs(w).max(1)
    if fmt == "e4m3":
        byte = np.frexp(amax)[1] - 1 + 127 - 7
    else:
        mant, ex = np.frexp(amax / 6.0)
        byte = np.where(mant > 0.5, ex, ex - 1) + 127
    byte = np.clip(np.where(amax > 0, byte, 1), 1, 254)
    scaled = (w * np.exp2(127.0 - byte)[:, None, :]).reshape(k, n).astype(np.float32)
    by_word = np.ascontiguousarray(scaled.reshape(k // 512, 128, 4, n).transpose(0, 1, 3, 2))
    if fmt == "e4m3":
        words = by_word.astype(ml_dtypes.float8_e4m3fn).view(np.uint8)
    else:
        c = by_word.astype(ml_dtypes.float4_e2m1fn).view(np.uint8) & 0xF
        words = c[..., 0::2] | (c[..., 1::2] << 4)
    return np.ascontiguousarray(words), np.ascontiguousarray(byte.astype(np.uint8).reshape(k // 512, 16, n))


def unpack_weight(words, scales, fmt):
    g, p, n, _ = words.shape
    if fmt == "e4m3":
        vals = np.ascontiguousarray(words).view(ml_dtypes.float8_e4m3fn).astype(np.float64)
    else:
        nib = np.empty((g, p, n, 4), np.uint8)
        nib[..., 0::2] = words & 0xF
        nib[..., 1::2] = words >> 4
        vals = E2M1[nib]
    vals = vals * np.repeat(np.exp2(scales.astype(np.float64) - 127.0), 8, axis=1)[..., None]
    return vals.transpose(0, 1, 3, 2).reshape(g * 512, n)

def pack4(w):
    words, scales = pack_weight(w, "e2m1")
    return words.reshape(words.shape[0], 128, -1), scales


def unpack4(words, scales):
    return unpack_weight(words.reshape(words.shape[0], 128, -1, 2), scales, "e2m1")


B, T, C, H, KH, D = 4, 128, 2048, 16, 4, 128
HALF = D // 2
RMS_EPS = 1e-6


def rms_norm(v, w):
    var = np.mean(v * v, axis=-1, keepdims=True)
    return v * (1.0 / np.sqrt(var + RMS_EPS)) * w


def rotary(v, cos, sin):
    v1, v2 = v[..., :HALF], v[..., HALF:]
    return np.concatenate([v1 * cos - v2 * sin, v1 * sin + v2 * cos], axis=-1)


def setup_inputs():
    s = mx_kscale(C)
    x = bf(np.random.standard_normal((B, T, C)) * s)
    cos = bf(np.random.uniform(0.0, 1.0, (1, T, 1, HALF)))
    sin = bf(np.random.uniform(0.0, 1.0, (1, T, 1, HALF)))
    wq_words, wq_scales = pack4(np.random.standard_normal((C, H * D)) / np.sqrt(C) / s[:, None])
    wk_words, wk_scales = pack4(np.random.standard_normal((C, KH * D)) / np.sqrt(C) / s[:, None])
    q_norm_w = bf(1.0 + 0.1 * np.random.standard_normal(D))
    k_norm_w = bf(1.0 + 0.1 * np.random.standard_normal(D))
    return {"x": x,
            "cos": cos,
            "sin": sin,
            "wq_words": wq_words,
            "wq_scales": wq_scales,
            "wk_words": wk_words,
            "wk_scales": wk_scales,
            "q_norm_w": q_norm_w,
            "k_norm_w": k_norm_w}


def reference(x, cos, sin, wq_words, wq_scales, wk_words, wk_scales, q_norm_w, k_norm_w):
    xq = mxq(f64(x), 2, "e5m2")
    q = (xq @ unpack4(wq_words, wq_scales)).reshape(B, T, H, D)
    k = (xq @ unpack4(wk_words, wk_scales)).reshape(B, T, KH, D)
    q = rms_norm(q, f64(q_norm_w))
    k = rms_norm(k, f64(k_norm_w))
    q = rotary(q, f64(cos), f64(sin))
    k = rotary(k, f64(cos), f64(sin))
    return q, k

@@ -1,0 +1,193 @@
+from contextlib import ExitStack
+
+import concourse.mybir as mybir
+from concourse.masks import make_identity
+
+B, T, C, H, KH, D = 4, 128, 2048, 16, 4, 128
+HALF = D // 2
+RMS_EPS = 1e-6
+FLOPS = 2 * B * T * C * (H + KH) * D
+
+F32 = mybir.dt.float32
+BF16 = mybir.dt.bfloat16
+I32 = mybir.dt.int32
+U32 = mybir.dt.uint32
+U8 = mybir.dt.uint8
+E5M2X4 = mybir.dt.float8_e5m2_x4
+E2M1X4 = mybir.dt.float4_e2m1fn_x4
+ACT = mybir.ActivationFunctionType
+ALU = mybir.AluOpType
+
+P = 128
+PASSES = C // 512
+N_TILE = 512
+HEADS = N_TILE // D
+VECTOR_ADDS = 1
+
+
+def tile_multiheadattention_pa_kernel(
+    tc, x, cos, sin, wq_words, wq_scales, wk_words, wk_scales, q_norm_w, k_norm_w, out_0, out_1
+):
+    nc = tc.nc
+    q_tiles = H * D // N_TILE
+
+    with ExitStack() as ctx:
+        keep = ctx.enter_context(tc.tile_pool(name="keep", bufs=1))
+        work = ctx.enter_context(tc.tile_pool(name="work", bufs=4))
+        psum = ctx.enter_context(tc.psum_pool(name="psum", bufs=1))
+        ctx.enter_context(tc.manual_schedule())
+
+        gain_rows = keep.tile([P, 2 * D], BF16)
+        ones = keep.tile([P, P], BF16)
+        ident = keep.tile([P, P], F32)
+        k_scale = keep.tile([P, PASSES, KH * D], U8, align_bytes=64)
+        q_scale = keep.tile([P, PASSES, H * D], U8, align_bytes=64)
+        cos_sb = keep.tile([P, HALF], BF16)
+        sin_sb = keep.tile([P, HALF], BF16)
+        signed_sin = keep.tile([P, 2, HALF], F32)
+        table = keep.tile([P, 2, 2, D], F32)
+
+        nc.vector.memset(gain_rows[:], 0.0)
+        nc.vector.memset(k_scale[:].bitcast(I32), 0)
+        nc.vector.memset(q_scale[:].bitcast(I32), 0)
+        make_identity(nc, ident[:])
+        nc.gpsimd.memset(ones[:], 1.0)
+
+        nc.scalar.dma_start(out=sin_sb[:], in_=sin.rearrange("a t b i -> t (a b i)"))
+        nc.scalar.dma_start(out=cos_sb[:], in_=cos.rearrange("a t b i -> t (a b i)"))
+        nc.scalar.dma_start(out=gain_rows[0:1, 0:D], in_=q_norm_w.rearrange("(a d) -> a d", a=1))
+        nc.scalar.dma_start(out=gain_rows[0:1, D : 2 * D], in_=k_norm_w.rearrange("(a d) -> a d", a=1))
+
+        x_sb = []
+        for b in range(B):
+            x_tile = keep.tile([P, C], BF16, name="x_%d" % b)
+            nc.sync.dma_start(out=x_tile[:], in_=x[b])
+            x_sb.append(x_tile)
+
+        def load_scales(plane, scales):
+            for r in range(4):
+                nc.sync.dma_start(
+                    out=plane[r:P:32, :, :].bitcast(I32),
+                    in_=scales[:, r:16:4, :].rearrange("g q n -> q g n").bitcast(I32),
+                )
+
+        def load_words(words, j, name):
+            w_tile = keep.tile([P, PASSES, 2 * N_TILE], U8, name=name, align_bytes=64)
+            nc.sync.dma_start(
+                out=w_tile[:].bitcast(I32),
+                in_=words[:, :, 2 * N_TILE * j : 2 * N_TILE * (j + 1)].rearrange("g p n -> p g n").bitcast(I32),
+            )
+            return w_tile
+
+        load_scales(k_scale, wk_scales)
+        k_words = load_words(wk_words, 0, "wk")
+        load_scales(q_scale, wq_scales)
+        q_words = [load_words(wq_words, j, "wq_%d" % j) for j in range(q_tiles)]
+
+        nc.scalar.activation(out=signed_sin[:, 0, :], in_=sin_sb[:], func=ACT.Copy)
+        nc.scalar.activation(out=signed_sin[:, 1, :], in_=sin_sb[:], func=ACT.Copy, scale=-1.0)
+
+        split = {}
+        grouped = {}
+        codes = {}
+        x_scale = {}
+
+        def split_words(b):
+            split[b] = keep.tile([P, PASSES, 2, P], F32, name="split_%d" % b)
+            nc.vector.tensor_copy(
+                out=split[b][:], in_=x_sb[b][:].bitcast(F32).rearrange("p (g w u) -> p g u w", g=PASSES, u=2)
+            )
+
+        def transpose(b):
+            grouped[b] = keep.tile([P, C], BF16, name="grouped_%d" % b, align_bytes=64)
+            words = grouped[b][:].bitcast(F32).rearrange("p (g r u) -> p g r u", g=PASSES, u=2)
+            for g0 in range(0, PASSES, 2):
+                bank = psum.tile([P, 2, 2, P], F32, name="xt", bufs=2)
+                for g in range(2):
+                    for u in range(2):
+                        nc.tensor.transpose(bank[:, g, u, :], split[b][:, g0 + g, u, :], ident[:])
+                nc.scalar.copy(out=words[:, g0 : g0 + 2], in_=bank[:].rearrange("p g u r -> p g r u"))
+
+        def quantize(b):
+            codes[b] = keep.tile([P, PASSES * P], U32, name="codes_%d" % b, align_bytes=64)
+            x_scale[b] = keep.tile([P, PASSES * P], U8, name="x_scale_%d" % b, align_bytes=64)
+            nc.vector.quantize_mx(out=codes[b][:].bitcast(E5M2X4), scales=x_scale[b][:], in_=grouped[b][:])
+
+        def build_table():
+            gains = psum.tile([P, 2, D], F32, name="acc", bufs=6)
+            nc.tensor.matmul(
+                gains[:].rearrange("p a d -> p (a d)"), lhsT=ones[:], rhs=gain_rows[:], start=True, stop=True
+            )
+            nc.vector.tensor_tensor(
+                out=table[:, :, 0, :].rearrange("p a (h i) -> p a h i", h=2),
+                in0=gains[:].rearrange("p a (h i) -> p a h i", h=2),
+                in1=cos_sb[:].unsqueeze(1).unsqueeze(1).to_broadcast([P, 2, 2, HALF]),
+                op=ALU.mult,
+            )
+            nc.vector.tensor_tensor(
+                out=table[:, :, 1, :],
+                in0=gains[:],
+                in1=signed_sin[:].rearrange("p h i -> p (h i)").unsqueeze(1).to_broadcast([P, 2, D]),
+                op=ALU.mult,
+            )
+
+        split_words(0)
+        transpose(0)
+        split_words(1)
+        build_table()
+        transpose(1)
+        for b in range(2, B):
+            split_words(b)
+            transpose(b)
+            quantize(b - 2)
+        quantize(B - 2)
+        quantize(B - 1)
+
+        k_out = out_1.rearrange("b t h d -> b t (h d)")
+        q_out = out_0.rearrange("b t h d -> b t (h d)")
+        jobs = [(b, k_words, k_scale, 0, 1, k_out) for b in range(B)]
+        jobs += [(b, q_words[j], q_scale, j, 0, q_out) for j in range(q_tiles) for b in range(B)]
+
+        for n, (b, w_tile, plane, j, which, dest) in enumerate(jobs):
+            cols = slice(N_TILE * j, N_TILE * (j + 1))
+            acc = psum.tile([P, N_TILE], F32, name="acc", bufs=6)
+            for g in range(PASSES):
+                nc.tensor.matmul_mx(
+                    out=acc[:],
+                    lhsT=codes[b][:, P * g : P * (g + 1)].bitcast(E5M2X4),
+                    lhsT_scale=x_scale[b][:, P * g : P * (g + 1)],
+                    rhs=w_tile[:, g, :].bitcast(E2M1X4),
+                    rhs_scale=plane[:, g, cols],
+                    start=(g == 0),
+                    stop=(g == PASSES - 1),
+                )
+            squares = work.tile([P, N_TILE], F32, bufs=2)
+            sums = work.tile([P, HEADS], F32)
+            rstd = work.tile([P, HEADS], F32)
+            for h in range(HEADS):
+                nc.scalar.activation(
+                    out=squares[:, D * h : D * (h + 1)],
+                    in_=acc[:, D * h : D * (h + 1)],
+                    func=ACT.Square,
+                    accum_out=sums[:, h : h + 1],
+                )
+            nc.scalar.activation(out=rstd[:], in_=sums[:], func=ACT.Abs_reciprocal_sqrt, scale=1.0 / D, bias=RMS_EPS)
+            prod = work.tile([P, 2, HEADS, D], F32)
+            for h in range(HEADS):
+                nc.vector.scalar_tensor_tensor(
+                    out=prod[:, :, h, :],
+                    in0=acc[:, D * h : D * (h + 1)].unsqueeze(1).to_broadcast([P, 2, D]),
+                    scalar=rstd[:, h : h + 1],
+                    in1=table[:, which],
+                    op0=ALU.mult,
+                    op1=ALU.mult,
+                )
+            result = work.tile([P, HEADS, 2, HALF], F32, bufs=6)
+            adder = nc.vector if n >= len(jobs) - VECTOR_ADDS else nc.gpsimd
+            adder.tensor_tensor(
+                out=result[:],
+                in0=prod[:, 0].rearrange("p h (s i) -> p h s i", s=2),
+                in1=prod[:, 1].rearrange("p h (s i) -> p h s i", s=2)[:, :, ::-1, :],
+                op=ALU.add,
+            )
+            nc.sync.dma_start(out=dest[b, :, cols], in_=result[:].rearrange("p h s i -> p (h s i)"))

@@ -22,7 +22,8 @@ P = 128
 PASSES = C // 512
 N_TILE = 512
 HEADS = N_TILE // D
-VECTOR_ADDS = 1
+TRANSPOSE_AFTER = 3
+VECTOR_PAIRS = 2
 
 
 def tile_multiheadattention_pa_kernel(
@@ -41,7 +42,8 @@ def tile_multiheadattention_pa_kernel(
         ones = keep.tile([P, P], BF16)
         ident = keep.tile([P, P], F32)
         k_scale = keep.tile([P, PASSES, KH * D], U8, align_bytes=64)
-        q_scale = keep.tile([P, PASSES, H * D], U8, align_bytes=64)
+        q_scale_lo = keep.tile([P, PASSES, H * D // 2], U8, align_bytes=64)
+        q_scale_hi = keep.tile([P, PASSES, H * D // 2], U8, align_bytes=64)
         cos_sb = keep.tile([P, HALF], BF16)
         sin_sb = keep.tile([P, HALF], BF16)
         signed_sin = keep.tile([P, 2, HALF], F32)
@@ -49,7 +51,8 @@ def tile_multiheadattention_pa_kernel(
 
         nc.vector.memset(gain_rows[:], 0.0)
         nc.vector.memset(k_scale[:].bitcast(I32), 0)
-        nc.vector.memset(q_scale[:].bitcast(I32), 0)
+        nc.vector.memset(q_scale_lo[:].bitcast(I32), 0)
+        nc.vector.memset(q_scale_hi[:].bitcast(I32), 0)
         make_identity(nc, ident[:])
         nc.gpsimd.memset(ones[:], 1.0)
 
@@ -58,11 +61,11 @@ def tile_multiheadattention_pa_kernel(
         nc.scalar.dma_start(out=gain_rows[0:1, 0:D], in_=q_norm_w.rearrange("(a d) -> a d", a=1))
         nc.scalar.dma_start(out=gain_rows[0:1, D : 2 * D], in_=k_norm_w.rearrange("(a d) -> a d", a=1))
 
-        x_sb = []
-        for b in range(B):
-            x_tile = keep.tile([P, C], BF16, name="x_%d" % b)
-            nc.sync.dma_start(out=x_tile[:], in_=x[b])
-            x_sb.append(x_tile)
+        x_sb = {}
+
+        def load_x(b):
+            x_sb[b] = keep.tile([P, C], BF16, name="x_%d" % b)
+            nc.sync.dma_start(out=x_sb[b][:], in_=x[b])
 
         def load_scales(plane, scales):
             for r in range(4):
@@ -79,45 +82,57 @@ def tile_multiheadattention_pa_kernel(
             )
             return w_tile
 
+        load_x(0)
+        load_x(1)
         load_scales(k_scale, wk_scales)
         k_words = load_words(wk_words, 0, "wk")
-        load_scales(q_scale, wq_scales)
-        q_words = [load_words(wq_words, j, "wq_%d" % j) for j in range(q_tiles)]
+        load_scales(q_scale_lo, wq_scales[:, :, : H * D // 2])
+        q_words = [load_words(wq_words, j, "wq_%d" % j) for j in range(2)]
+        load_scales(q_scale_hi, wq_scales[:, :, H * D // 2 :])
+        q_words += [load_words(wq_words, j, "wq_%d" % j) for j in range(2, q_tiles)]
+        load_x(2)
+        load_x(3)
 
         nc.scalar.activation(out=signed_sin[:, 0, :], in_=sin_sb[:], func=ACT.Copy)
         nc.scalar.activation(out=signed_sin[:, 1, :], in_=sin_sb[:], func=ACT.Copy, scale=-1.0)
 
-        split = {}
-        grouped = {}
-        codes = {}
-        x_scale = {}
+        grouped = keep.tile([P, B, C], BF16, align_bytes=64)
+        codes = keep.tile([P, B, PASSES * P], U32, align_bytes=64)
+        x_scale = keep.tile([P, B, PASSES * P], U8, align_bytes=64)
+
+        def word_view(b):
+            return x_sb[b][:].bitcast(F32).rearrange("p (g w u) -> p g u w", g=PASSES, u=2)
 
         def split_words(b):
-            split[b] = keep.tile([P, PASSES, 2, P], F32, name="split_%d" % b)
-            nc.vector.tensor_copy(
-                out=split[b][:], in_=x_sb[b][:].bitcast(F32).rearrange("p (g w u) -> p g u w", g=PASSES, u=2)
-            )
+            split = keep.tile([P, PASSES, 2, P], F32, name="split_%d" % b)
+            for g0 in range(0, PASSES, 2):
+                nc.vector.tensor_copy(out=split[:, g0 : g0 + 2], in_=word_view(b)[:, g0 : g0 + 2])
+            return split
 
-        def transpose(b):
-            grouped[b] = keep.tile([P, C], BF16, name="grouped_%d" % b, align_bytes=64)
-            words = grouped[b][:].bitcast(F32).rearrange("p (g r u) -> p g r u", g=PASSES, u=2)
+        def transpose(b, source):
+            words = grouped[:, b, :].bitcast(F32).rearrange("p (g r u) -> p g r u", g=PASSES, u=2)
             for g0 in range(0, PASSES, 2):
                 bank = psum.tile([P, 2, 2, P], F32, name="xt", bufs=2)
                 for g in range(2):
                     for u in range(2):
-                        nc.tensor.transpose(bank[:, g, u, :], split[b][:, g0 + g, u, :], ident[:])
+                        nc.tensor.transpose(bank[:, g, u, :], source[:, g0 + g, u, :], ident[:])
                 nc.scalar.copy(out=words[:, g0 : g0 + 2], in_=bank[:].rearrange("p g u r -> p g r u"))
 
-        def quantize(b):
-            codes[b] = keep.tile([P, PASSES * P], U32, name="codes_%d" % b, align_bytes=64)
-            x_scale[b] = keep.tile([P, PASSES * P], U8, name="x_scale_%d" % b, align_bytes=64)
-            nc.vector.quantize_mx(out=codes[b][:].bitcast(E5M2X4), scales=x_scale[b][:], in_=grouped[b][:])
+        def quantize(first, last):
+            nc.vector.quantize_mx(
+                out=codes[:].rearrange("p b n -> p (b n)")[:, P * first : P * last].bitcast(E5M2X4),
+                scales=x_scale[:].rearrange("p b n -> p (b n)")[:, P * first : P * last],
+                in_=grouped[:].rearrange("p b n -> p (b n)")[:, 4 * P * first : 4 * P * last],
+            )
 
-        def build_table():
+        def spread_gains():
             gains = psum.tile([P, 2, D], F32, name="acc", bufs=6)
             nc.tensor.matmul(
                 gains[:].rearrange("p a d -> p (a d)"), lhsT=ones[:], rhs=gain_rows[:], start=True, stop=True
             )
+            return gains
+
+        def build_table(gains):
             nc.vector.tensor_tensor(
                 out=table[:, :, 0, :].rearrange("p a (h i) -> p a h i", h=2),
                 in0=gains[:].rearrange("p a (h i) -> p a h i", h=2),
@@ -131,39 +146,21 @@ def tile_multiheadattention_pa_kernel(
                 op=ALU.mult,
             )
 
-        split_words(0)
-        transpose(0)
-        split_words(1)
-        build_table()
-        transpose(1)
-        for b in range(2, B):
-            split_words(b)
-            transpose(b)
-            quantize(b - 2)
-        quantize(B - 2)
-        quantize(B - 1)
-
-        k_out = out_1.rearrange("b t h d -> b t (h d)")
-        q_out = out_0.rearrange("b t h d -> b t (h d)")
-        jobs = [(b, k_words, k_scale, 0, 1, k_out) for b in range(B)]
-        jobs += [(b, q_words[j], q_scale, j, 0, q_out) for j in range(q_tiles) for b in range(B)]
-
-        for n, (b, w_tile, plane, j, which, dest) in enumerate(jobs):
-            cols = slice(N_TILE * j, N_TILE * (j + 1))
+        def project(b, w_tile, plane_cols):
             acc = psum.tile([P, N_TILE], F32, name="acc", bufs=6)
             for g in range(PASSES):
                 nc.tensor.matmul_mx(
                     out=acc[:],
-                    lhsT=codes[b][:, P * g : P * (g + 1)].bitcast(E5M2X4),
-                    lhsT_scale=x_scale[b][:, P * g : P * (g + 1)],
+                    lhsT=codes[:, b, P * g : P * (g + 1)].bitcast(E5M2X4),
+                    lhsT_scale=x_scale[:, b, P * g : P * (g + 1)],
                     rhs=w_tile[:, g, :].bitcast(E2M1X4),
-                    rhs_scale=plane[:, g, cols],
+                    rhs_scale=plane_cols[:, g, :],
                     start=(g == 0),
                     stop=(g == PASSES - 1),
                 )
             squares = work.tile([P, N_TILE], F32, bufs=2)
-            sums = work.tile([P, HEADS], F32)
-            rstd = work.tile([P, HEADS], F32)
+            sums = work.tile([P, HEADS], F32, bufs=6)
+            rstd = work.tile([P, HEADS], F32, bufs=6)
             for h in range(HEADS):
                 nc.scalar.activation(
                     out=squares[:, D * h : D * (h + 1)],
@@ -172,7 +169,9 @@ def tile_multiheadattention_pa_kernel(
                     accum_out=sums[:, h : h + 1],
                 )
             nc.scalar.activation(out=rstd[:], in_=sums[:], func=ACT.Abs_reciprocal_sqrt, scale=1.0 / D, bias=RMS_EPS)
-            prod = work.tile([P, 2, HEADS, D], F32)
+            return acc, rstd
+
+        def products(acc, rstd, which, prod):
             for h in range(HEADS):
                 nc.vector.scalar_tensor_tensor(
                     out=prod[:, :, h, :],
@@ -182,12 +181,52 @@ def tile_multiheadattention_pa_kernel(
                     op0=ALU.mult,
                     op1=ALU.mult,
                 )
-            result = work.tile([P, HEADS, 2, HALF], F32, bufs=6)
-            adder = nc.vector if n >= len(jobs) - VECTOR_ADDS else nc.gpsimd
-            adder.tensor_tensor(
-                out=result[:],
+
+        def add_halves(engine, result, prod):
+            engine.tensor_tensor(
+                out=result.rearrange("p h (s i) -> p h s i", s=2),
                 in0=prod[:, 0].rearrange("p h (s i) -> p h s i", s=2),
                 in1=prod[:, 1].rearrange("p h (s i) -> p h s i", s=2)[:, :, ::-1, :],
                 op=ALU.add,
             )
-            nc.sync.dma_start(out=dest[b, :, cols], in_=result[:].rearrange("p h s i -> p (h s i)"))
+
+        gains = spread_gains()
+        transpose(0, split_words(0))
+        build_table(gains)
+        transpose(1, split_words(1))
+        for first in range(0, 2 * PASSES, 2):
+            quantize(first, first + 2)
+
+        k_out = out_1.rearrange("b t h d -> t b (h d)")
+        q_out = out_0.rearrange("b t h d -> t b (h d)")
+        column_tiles = [(k_words, k_scale, 1, k_out)]
+        for j in range(q_tiles):
+            plane = (q_scale_lo, q_scale_hi)[j // 2]
+            column_tiles.append(
+                (q_words[j], plane[:, :, N_TILE * (j % 2) : N_TILE * (j % 2 + 1)], 0, q_out[:, :, N_TILE * j : N_TILE * (j + 1)])
+            )
+        jobs = [(b0, tile) for b0 in (0, 2) for tile in column_tiles]
+
+        last_adds = []
+        for n, (b0, (w_tile, plane_cols, which, dest)) in enumerate(jobs):
+            prod = work.tile([P, 2, 2 * HEADS, D], F32, bufs=4)
+            result = work.tile([P, 2 * HEADS, D], F32, bufs=4)
+            first = project(b0, w_tile, plane_cols)
+            second = project(b0 + 1, w_tile, plane_cols)
+            if n == TRANSPOSE_AFTER:
+                transpose(2, word_view(2))
+                transpose(3, word_view(3))
+            products(*first, which, prod[:, :, :HEADS, :])
+            if n == TRANSPOSE_AFTER:
+                quantize(2 * PASSES, 4 * PASSES)
+            products(*second, which, prod[:, :, HEADS:, :])
+            if n < len(jobs) - VECTOR_PAIRS:
+                add_halves(nc.gpsimd, result[:], prod[:])
+                nc.sync.dma_start(out=dest[:, b0 : b0 + 2, :], in_=result[:].rearrange("p (b h) d -> p b (h d)", b=2))
+            else:
+                last_adds.append((result, prod, dest[:, b0 : b0 + 2, :]))
+        for result, prod, dest in last_adds:
+            for e in range(2):
+                heads = slice(HEADS * e, HEADS * (e + 1))
+                add_halves(nc.vector, result[:, heads, :], prod[:, :, heads, :])
+                nc.sync.dma_start(out=dest[:, e, :], in_=result[:, heads, :].rearrange("p h d -> p (h d)"))

@@ -23,7 +23,7 @@ PASSES = C // 512
 N_TILE = 512
 HEADS = N_TILE // D
 TRANSPOSE_AFTER = 3
-VECTOR_PAIRS = 2
+SCALE_LAG = 3
 
 
 def tile_multiheadattention_pa_kernel(
@@ -57,9 +57,6 @@ def tile_multiheadattention_pa_kernel(
         nc.gpsimd.memset(ones[:], 1.0)
 
         nc.scalar.dma_start(out=sin_sb[:], in_=sin.rearrange("a t b i -> t (a b i)"))
-        nc.scalar.dma_start(out=cos_sb[:], in_=cos.rearrange("a t b i -> t (a b i)"))
-        nc.scalar.dma_start(out=gain_rows[0:1, 0:D], in_=q_norm_w.rearrange("(a d) -> a d", a=1))
-        nc.scalar.dma_start(out=gain_rows[0:1, D : 2 * D], in_=k_norm_w.rearrange("(a d) -> a d", a=1))
 
         x_sb = {}
 
@@ -86,6 +83,9 @@ def tile_multiheadattention_pa_kernel(
         load_x(1)
         load_scales(k_scale, wk_scales)
         k_words = load_words(wk_words, 0, "wk")
+        nc.sync.dma_start(out=gain_rows[0:1, 0:D], in_=q_norm_w.rearrange("(a d) -> a d", a=1))
+        nc.sync.dma_start(out=gain_rows[0:1, D : 2 * D], in_=k_norm_w.rearrange("(a d) -> a d", a=1))
+        nc.sync.dma_start(out=cos_sb[:], in_=cos.rearrange("a t b i -> t (a b i)"))
         load_scales(q_scale_lo, wq_scales[:, :, : H * D // 2])
         q_words = [load_words(wq_words, j, "wq_%d" % j) for j in range(2)]
         load_scales(q_scale_hi, wq_scales[:, :, H * D // 2 :])
@@ -146,7 +146,7 @@ def tile_multiheadattention_pa_kernel(
                 op=ALU.mult,
             )
 
-        def project(b, w_tile, plane_cols):
+        def project(b, w_tile, plane_cols, sums):
             acc = psum.tile([P, N_TILE], F32, name="acc", bufs=6)
             for g in range(PASSES):
                 nc.tensor.matmul_mx(
@@ -159,8 +159,6 @@ def tile_multiheadattention_pa_kernel(
                     stop=(g == PASSES - 1),
                 )
             squares = work.tile([P, N_TILE], F32, bufs=2)
-            sums = work.tile([P, HEADS], F32, bufs=6)
-            rstd = work.tile([P, HEADS], F32, bufs=6)
             for h in range(HEADS):
                 nc.scalar.activation(
                     out=squares[:, D * h : D * (h + 1)],
@@ -168,8 +166,15 @@ def tile_multiheadattention_pa_kernel(
                     func=ACT.Square,
                     accum_out=sums[:, h : h + 1],
                 )
-            nc.scalar.activation(out=rstd[:], in_=sums[:], func=ACT.Abs_reciprocal_sqrt, scale=1.0 / D, bias=RMS_EPS)
-            return acc, rstd
+            return acc
+
+        def plain_products(acc, which, prod):
+            nc.vector.tensor_tensor(
+                out=prod,
+                in0=acc[:].rearrange("p (h d) -> p h d", h=HEADS).unsqueeze(1).to_broadcast([P, 2, HEADS, D]),
+                in1=table[:, which].unsqueeze(2).to_broadcast([P, 2, HEADS, D]),
+                op=ALU.mult,
+            )
 
         def products(acc, rstd, which, prod):
             for h in range(HEADS):
@@ -190,9 +195,7 @@ def tile_multiheadattention_pa_kernel(
                 op=ALU.add,
             )
 
-        gains = spread_gains()
         transpose(0, split_words(0))
-        build_table(gains)
         transpose(1, split_words(1))
         for first in range(0, 2 * PASSES, 2):
             quantize(first, first + 2)
@@ -207,26 +210,54 @@ def tile_multiheadattention_pa_kernel(
             )
         jobs = [(b0, tile) for b0 in (0, 2) for tile in column_tiles]
 
-        last_adds = []
+        def scale_heads(result, rstd):
+            for h in range(HEADS):
+                nc.scalar.activation(out=result[:, h, :], in_=result[:, h, :], func=ACT.Copy, scale=rstd[:, h : h + 1])
+
+        def store(dest, result):
+            nc.sync.dma_start(out=dest, in_=result.rearrange("p (b h) d -> p b (h d)", h=HEADS))
+
+        lower, upper = slice(0, HEADS), slice(HEADS, 2 * HEADS)
+        last = len(jobs) - 1
+        unscaled = []
         for n, (b0, (w_tile, plane_cols, which, dest)) in enumerate(jobs):
             prod = work.tile([P, 2, 2 * HEADS, D], F32, bufs=4)
-            result = work.tile([P, 2 * HEADS, D], F32, bufs=4)
-            first = project(b0, w_tile, plane_cols)
-            second = project(b0 + 1, w_tile, plane_cols)
+            result = work.tile([P, 2 * HEADS, D], F32, bufs=6)
+            sums = work.tile([P, 2 * HEADS], F32, bufs=6)
+            rstd = work.tile([P, 2 * HEADS], F32, bufs=6)
+            first = project(b0, w_tile, plane_cols, sums[:, lower])
+            if n == 0:
+                build_table(spread_gains())
+            second = project(b0 + 1, w_tile, plane_cols, sums[:, upper])
+            nc.scalar.activation(out=rstd[:], in_=sums[:], func=ACT.Abs_reciprocal_sqrt, scale=1.0 / D, bias=RMS_EPS)
             if n == TRANSPOSE_AFTER:
                 transpose(2, word_view(2))
                 transpose(3, word_view(3))
-            products(*first, which, prod[:, :, :HEADS, :])
+            if n >= SCALE_LAG:
+                old_result, old_rstd, old_dest = unscaled.pop(0)
+                scale_heads(old_result, old_rstd)
+                store(old_dest, old_result[:])
+            if n < last:
+                plain_products(first, which, prod[:, :, lower, :])
+            else:
+                products(first, rstd[:, lower], which, prod[:, :, lower, :])
             if n == TRANSPOSE_AFTER:
                 quantize(2 * PASSES, 4 * PASSES)
-            products(*second, which, prod[:, :, HEADS:, :])
-            if n < len(jobs) - VECTOR_PAIRS:
+            products(second, rstd[:, upper], which, prod[:, :, upper, :])
+            if n < last - 1:
                 add_halves(nc.gpsimd, result[:], prod[:])
-                nc.sync.dma_start(out=dest[:, b0 : b0 + 2, :], in_=result[:].rearrange("p (b h) d -> p b (h d)", b=2))
-            else:
-                last_adds.append((result, prod, dest[:, b0 : b0 + 2, :]))
-        for result, prod, dest in last_adds:
-            for e in range(2):
-                heads = slice(HEADS * e, HEADS * (e + 1))
-                add_halves(nc.vector, result[:, heads, :], prod[:, :, heads, :])
-                nc.sync.dma_start(out=dest[:, e, :], in_=result[:, heads, :].rearrange("p h d -> p (h d)"))
+                unscaled.append((result, rstd, dest[:, b0 : b0 + 2, :]))
+            elif n < last:
+                add_halves(nc.gpsimd, result[:, lower, :], prod[:, :, lower, :])
+                add_halves(nc.gpsimd, result[:, upper, :], prod[:, :, upper, :])
+                closing = (result, rstd, dest)
+        for old_result, old_rstd, old_dest in unscaled:
+            scale_heads(old_result, old_rstd)
+            store(old_dest, old_result[:])
+        old_result, old_rstd, old_dest = closing
+        scale_heads(old_result, old_rstd)
+        store(old_dest[:, b0 : b0 + 1, :], old_result[:, lower, :])
+        store(old_dest[:, b0 + 1 : b0 + 2, :], old_result[:, upper, :])
+        for e, heads in enumerate((lower, upper)):
+            add_halves(nc.vector, result[:, heads, :], prod[:, :, heads, :])
+            store(dest[:, b0 + e : b0 + e + 1, :], result[:, heads, :])

@@ -22,8 +22,9 @@ P = 128
 PASSES = C // 512
 N_TILE = 512
 HEADS = N_TILE // D
-TRANSPOSE_AFTER = 3
+TRANSPOSE_AFTER = 2
 SCALE_LAG = 3
+PLAIN_PAIRS = (0, 3, 5, 6, 7)
 
 
 def tile_multiheadattention_pa_kernel(
@@ -88,10 +89,10 @@ def tile_multiheadattention_pa_kernel(
         nc.sync.dma_start(out=cos_sb[:], in_=cos.rearrange("a t b i -> t (a b i)"))
         load_scales(q_scale_lo, wq_scales[:, :, : H * D // 2])
         q_words = [load_words(wq_words, j, "wq_%d" % j) for j in range(2)]
-        load_scales(q_scale_hi, wq_scales[:, :, H * D // 2 :])
-        q_words += [load_words(wq_words, j, "wq_%d" % j) for j in range(2, q_tiles)]
         load_x(2)
         load_x(3)
+        load_scales(q_scale_hi, wq_scales[:, :, H * D // 2 :])
+        q_words += [load_words(wq_words, j, "wq_%d" % j) for j in range(2, q_tiles)]
 
         nc.scalar.activation(out=signed_sin[:, 0, :], in_=sin_sb[:], func=ACT.Copy)
         nc.scalar.activation(out=signed_sin[:, 1, :], in_=sin_sb[:], func=ACT.Copy, scale=-1.0)
@@ -210,17 +211,24 @@ def tile_multiheadattention_pa_kernel(
             )
         jobs = [(b0, tile) for b0 in (0, 2) for tile in column_tiles]
 
-        def scale_heads(result, rstd):
-            for h in range(HEADS):
-                nc.scalar.activation(out=result[:, h, :], in_=result[:, h, :], func=ACT.Copy, scale=rstd[:, h : h + 1])
+        def inverse_rms(rstd, sums):
+            nc.scalar.activation(out=rstd, in_=sums, func=ACT.Abs_reciprocal_sqrt, scale=1.0 / D, bias=RMS_EPS)
 
         def store(dest, result):
             nc.sync.dma_start(out=dest, in_=result.rearrange("p (b h) d -> p b (h d)", h=HEADS))
 
+        def scale_and_store(result, rstd, dest):
+            for h in range(HEADS):
+                nc.scalar.activation(out=result[:, h, :], in_=result[:, h, :], func=ACT.Copy, scale=rstd[:, h : h + 1])
+            store(dest[:, 0:1, :], result[:, lower, :])
+
         lower, upper = slice(0, HEADS), slice(HEADS, 2 * HEADS)
         last = len(jobs) - 1
-        unscaled = []
-        for n, (b0, (w_tile, plane_cols, which, dest)) in enumerate(jobs):
+        unscaled = {}
+        closing = []
+        for n, (b0, (w_tile, plane_cols, which, columns)) in enumerate(jobs):
+            plain = n in PLAIN_PAIRS
+            dest = columns[:, b0 : b0 + 2, :]
             prod = work.tile([P, 2, 2 * HEADS, D], F32, bufs=4)
             result = work.tile([P, 2 * HEADS, D], F32, bufs=6)
             sums = work.tile([P, 2 * HEADS], F32, bufs=6)
@@ -228,36 +236,38 @@ def tile_multiheadattention_pa_kernel(
             first = project(b0, w_tile, plane_cols, sums[:, lower])
             if n == 0:
                 build_table(spread_gains())
-            second = project(b0 + 1, w_tile, plane_cols, sums[:, upper])
-            nc.scalar.activation(out=rstd[:], in_=sums[:], func=ACT.Abs_reciprocal_sqrt, scale=1.0 / D, bias=RMS_EPS)
+            if not plain:
+                inverse_rms(rstd[:, lower], sums[:, lower])
             if n == TRANSPOSE_AFTER:
                 transpose(2, word_view(2))
+            second = project(b0 + 1, w_tile, plane_cols, sums[:, upper])
+            if plain:
+                inverse_rms(rstd[:], sums[:])
+            else:
+                inverse_rms(rstd[:, upper], sums[:, upper])
+            if n == TRANSPOSE_AFTER:
                 transpose(3, word_view(3))
-            if n >= SCALE_LAG:
-                old_result, old_rstd, old_dest = unscaled.pop(0)
-                scale_heads(old_result, old_rstd)
-                store(old_dest, old_result[:])
-            if n < last:
+            if n - SCALE_LAG in unscaled:
+                scale_and_store(*unscaled.pop(n - SCALE_LAG))
+            if plain:
                 plain_products(first, which, prod[:, :, lower, :])
             else:
                 products(first, rstd[:, lower], which, prod[:, :, lower, :])
+            products(second, rstd[:, upper], which, prod[:, :, upper, :])
             if n == TRANSPOSE_AFTER:
                 quantize(2 * PASSES, 4 * PASSES)
-            products(second, rstd[:, upper], which, prod[:, :, upper, :])
             if n < last - 1:
                 add_halves(nc.gpsimd, result[:], prod[:])
-                unscaled.append((result, rstd, dest[:, b0 : b0 + 2, :]))
-            elif n < last:
-                add_halves(nc.gpsimd, result[:, lower, :], prod[:, :, lower, :])
-                add_halves(nc.gpsimd, result[:, upper, :], prod[:, :, upper, :])
-                closing = (result, rstd, dest)
-        for old_result, old_rstd, old_dest in unscaled:
-            scale_heads(old_result, old_rstd)
-            store(old_dest, old_result[:])
-        old_result, old_rstd, old_dest = closing
-        scale_heads(old_result, old_rstd)
-        store(old_dest[:, b0 : b0 + 1, :], old_result[:, lower, :])
-        store(old_dest[:, b0 + 1 : b0 + 2, :], old_result[:, upper, :])
-        for e, heads in enumerate((lower, upper)):
-            add_halves(nc.vector, result[:, heads, :], prod[:, :, heads, :])
-            store(dest[:, b0 + e : b0 + e + 1, :], result[:, heads, :])
+                if plain:
+                    store(dest[:, 1:2, :], result[:, upper, :])
+                    unscaled[n] = (result, rstd, dest)
+                else:
+                    store(dest, result[:])
+            else:
+                closing.append((result[:, lower, :], prod[:, :, lower, :], dest[:, 0:1, :]))
+                closing.append((result[:, upper, :], prod[:, :, upper, :], dest[:, 1:2, :]))
+        for waiting in unscaled.values():
+            scale_and_store(*waiting)
+        for i, (result, prod, dest) in enumerate(closing):
+            add_halves(nc.gpsimd if i == 0 else nc.vector, result, prod)
+            store(dest, result)

@@ -40,7 +40,7 @@ def tile_multiheadattention_pa_kernel(
         ctx.enter_context(tc.manual_schedule())
 
         gain_rows = keep.tile([P, 2 * D], BF16)
-        ones = keep.tile([P, P], BF16)
+        ones = keep.tile([P, N_TILE], BF16)
         ident = keep.tile([P, P], F32)
         k_scale = keep.tile([P, PASSES, KH * D], U8, align_bytes=64)
         q_scale_lo = keep.tile([P, PASSES, H * D // 2], U8, align_bytes=64)
@@ -129,7 +129,7 @@ def tile_multiheadattention_pa_kernel(
         def spread_gains():
             gains = psum.tile([P, 2, D], F32, name="acc", bufs=6)
             nc.tensor.matmul(
-                gains[:].rearrange("p a d -> p (a d)"), lhsT=ones[:], rhs=gain_rows[:], start=True, stop=True
+                gains[:].rearrange("p a d -> p (a d)"), lhsT=ones[:, :P], rhs=gain_rows[:], start=True, stop=True
             )
             return gains
 
@@ -196,8 +196,15 @@ def tile_multiheadattention_pa_kernel(
                 op=ALU.add,
             )
 
+        def warm_up(count):
+            unread = psum.tile([P, N_TILE], F32, name="acc", bufs=6)
+            for i in range(count):
+                nc.tensor.matmul(unread[:], lhsT=ones[:, :P], rhs=ones[:], start=(i == 0), stop=(i == count - 1))
+
+        warm_up(6)
         transpose(0, split_words(0))
         transpose(1, split_words(1))
+        warm_up(2)
         for first in range(0, 2 * PASSES, 2):
             quantize(first, first + 2)
 

from contextlib import ExitStack

import concourse.mybir as mybir
from concourse.masks import make_identity

B, T, C, H, KH, D = 4, 128, 2048, 16, 4, 128
HALF = D // 2
RMS_EPS = 1e-6
FLOPS = 2 * B * T * C * (H + KH) * D

F32 = mybir.dt.float32
BF16 = mybir.dt.bfloat16
I32 = mybir.dt.int32
U32 = mybir.dt.uint32
U8 = mybir.dt.uint8
E5M2X4 = mybir.dt.float8_e5m2_x4
E2M1X4 = mybir.dt.float4_e2m1fn_x4
ACT = mybir.ActivationFunctionType
ALU = mybir.AluOpType

P = 128
PASSES = C // 512
N_TILE = 512
HEADS = N_TILE // D
TRANSPOSE_AFTER = 2
SCALE_LAG = 3
PLAIN_PAIRS = (0, 3, 5, 6, 7)


def tile_multiheadattention_pa_kernel(
    tc, x, cos, sin, wq_words, wq_scales, wk_words, wk_scales, q_norm_w, k_norm_w, out_0, out_1
):
    nc = tc.nc
    q_tiles = H * D // N_TILE

    with ExitStack() as ctx:
        keep = ctx.enter_context(tc.tile_pool(name="keep", bufs=1))
        work = ctx.enter_context(tc.tile_pool(name="work", bufs=4))
        psum = ctx.enter_context(tc.psum_pool(name="psum", bufs=1))
        ctx.enter_context(tc.manual_schedule())

        gain_rows = keep.tile([P, 2 * D], BF16)
        ones = keep.tile([P, N_TILE], BF16)
        ident = keep.tile([P, P], F32)
        k_scale = keep.tile([P, PASSES, KH * D], U8, align_bytes=64)
        q_scale_lo = keep.tile([P, PASSES, H * D // 2], U8, align_bytes=64)
        q_scale_hi = keep.tile([P, PASSES, H * D // 2], U8, align_bytes=64)
        cos_sb = keep.tile([P, HALF], BF16)
        sin_sb = keep.tile([P, HALF], BF16)
        signed_sin = keep.tile([P, 2, HALF], F32)
        table = keep.tile([P, 2, 2, D], F32)

        nc.vector.memset(gain_rows[:], 0.0)
        nc.vector.memset(k_scale[:].bitcast(I32), 0)
        nc.vector.memset(q_scale_lo[:].bitcast(I32), 0)
        nc.vector.memset(q_scale_hi[:].bitcast(I32), 0)
        make_identity(nc, ident[:])
        nc.gpsimd.memset(ones[:], 1.0)

        nc.scalar.dma_start(out=sin_sb[:], in_=sin.rearrange("a t b i -> t (a b i)"))

        x_sb = {}

        def load_x(b):
            x_sb[b] = keep.tile([P, C], BF16, name="x_%d" % b)
            nc.sync.dma_start(out=x_sb[b][:], in_=x[b])

        def load_scales(plane, scales):
            for r in range(4):
                nc.sync.dma_start(
                    out=plane[r:P:32, :, :].bitcast(I32),
                    in_=scales[:, r:16:4, :].rearrange("g q n -> q g n").bitcast(I32),
                )

        def load_words(words, j, name):
            w_tile = keep.tile([P, PASSES, 2 * N_TILE], U8, name=name, align_bytes=64)
            nc.sync.dma_start(
                out=w_tile[:].bitcast(I32),
                in_=words[:, :, 2 * N_TILE * j : 2 * N_TILE * (j + 1)].rearrange("g p n -> p g n").bitcast(I32),
            )
            return w_tile

        load_x(0)
        load_x(1)
        load_scales(k_scale, wk_scales)
        k_words = load_words(wk_words, 0, "wk")
        nc.sync.dma_start(out=gain_rows[0:1, 0:D], in_=q_norm_w.rearrange("(a d) -> a d", a=1))
        nc.sync.dma_start(out=gain_rows[0:1, D : 2 * D], in_=k_norm_w.rearrange("(a d) -> a d", a=1))
        nc.sync.dma_start(out=cos_sb[:], in_=cos.rearrange("a t b i -> t (a b i)"))
        load_scales(q_scale_lo, wq_scales[:, :, : H * D // 2])
        q_words = [load_words(wq_words, j, "wq_%d" % j) for j in range(2)]
        load_x(2)
        load_x(3)
        load_scales(q_scale_hi, wq_scales[:, :, H * D // 2 :])
        q_words += [load_words(wq_words, j, "wq_%d" % j) for j in range(2, q_tiles)]

        nc.scalar.activation(out=signed_sin[:, 0, :], in_=sin_sb[:], func=ACT.Copy)
        nc.scalar.activation(out=signed_sin[:, 1, :], in_=sin_sb[:], func=ACT.Copy, scale=-1.0)

        grouped = keep.tile([P, B, C], BF16, align_bytes=64)
        codes = keep.tile([P, B, PASSES * P], U32, align_bytes=64)
        x_scale = keep.tile([P, B, PASSES * P], U8, align_bytes=64)

        def word_view(b):
            return x_sb[b][:].bitcast(F32).rearrange("p (g w u) -> p g u w", g=PASSES, u=2)

        def split_words(b):
            split = keep.tile([P, PASSES, 2, P], F32, name="split_%d" % b)
            for g0 in range(0, PASSES, 2):
                nc.vector.tensor_copy(out=split[:, g0 : g0 + 2], in_=word_view(b)[:, g0 : g0 + 2])
            return split

        def transpose(b, source):
            words = grouped[:, b, :].bitcast(F32).rearrange("p (g r u) -> p g r u", g=PASSES, u=2)
            for g0 in range(0, PASSES, 2):
                bank = psum.tile([P, 2, 2, P], F32, name="xt", bufs=2)
                for g in range(2):
                    for u in range(2):
                        nc.tensor.transpose(bank[:, g, u, :], source[:, g0 + g, u, :], ident[:])
                nc.scalar.copy(out=words[:, g0 : g0 + 2], in_=bank[:].rearrange("p g u r -> p g r u"))

        def quantize(first, last):
            nc.vector.quantize_mx(
                out=codes[:].rearrange("p b n -> p (b n)")[:, P * first : P * last].bitcast(E5M2X4),
                scales=x_scale[:].rearrange("p b n -> p (b n)")[:, P * first : P * last],
                in_=grouped[:].rearrange("p b n -> p (b n)")[:, 4 * P * first : 4 * P * last],
            )

        def spread_gains():
            gains = psum.tile([P, 2, D], F32, name="acc", bufs=6)
            nc.tensor.matmul(
                gains[:].rearrange("p a d -> p (a d)"), lhsT=ones[:, :P], rhs=gain_rows[:], start=True, stop=True
            )
            return gains

        def build_table(gains):
            nc.vector.tensor_tensor(
                out=table[:, :, 0, :].rearrange("p a (h i) -> p a h i", h=2),
                in0=gains[:].rearrange("p a (h i) -> p a h i", h=2),
                in1=cos_sb[:].unsqueeze(1).unsqueeze(1).to_broadcast([P, 2, 2, HALF]),
                op=ALU.mult,
            )
            nc.vector.tensor_tensor(
                out=table[:, :, 1, :],
                in0=gains[:],
                in1=signed_sin[:].rearrange("p h i -> p (h i)").unsqueeze(1).to_broadcast([P, 2, D]),
                op=ALU.mult,
            )

        def project(b, w_tile, plane_cols, sums):
            acc = psum.tile([P, N_TILE], F32, name="acc", bufs=6)
            for g in range(PASSES):
                nc.tensor.matmul_mx(
                    out=acc[:],
                    lhsT=codes[:, b, P * g : P * (g + 1)].bitcast(E5M2X4),
                    lhsT_scale=x_scale[:, b, P * g : P * (g + 1)],
                    rhs=w_tile[:, g, :].bitcast(E2M1X4),
                    rhs_scale=plane_cols[:, g, :],
                    start=(g == 0),
                    stop=(g == PASSES - 1),
                )
            squares = work.tile([P, N_TILE], F32, bufs=2)
            for h in range(HEADS):
                nc.scalar.activation(
                    out=squares[:, D * h : D * (h + 1)],
                    in_=acc[:, D * h : D * (h + 1)],
                    func=ACT.Square,
                    accum_out=sums[:, h : h + 1],
                )
            return acc

        def plain_products(acc, which, prod):
            nc.vector.tensor_tensor(
                out=prod,
                in0=acc[:].rearrange("p (h d) -> p h d", h=HEADS).unsqueeze(1).to_broadcast([P, 2, HEADS, D]),
                in1=table[:, which].unsqueeze(2).to_broadcast([P, 2, HEADS, D]),
                op=ALU.mult,
            )

        def products(acc, rstd, which, prod):
            for h in range(HEADS):
                nc.vector.scalar_tensor_tensor(
                    out=prod[:, :, h, :],
                    in0=acc[:, D * h : D * (h + 1)].unsqueeze(1).to_broadcast([P, 2, D]),
                    scalar=rstd[:, h : h + 1],
                    in1=table[:, which],
                    op0=ALU.mult,
                    op1=ALU.mult,
                )

        def add_halves(engine, result, prod):
            engine.tensor_tensor(
                out=result.rearrange("p h (s i) -> p h s i", s=2),
                in0=prod[:, 0].rearrange("p h (s i) -> p h s i", s=2),
                in1=prod[:, 1].rearrange("p h (s i) -> p h s i", s=2)[:, :, ::-1, :],
                op=ALU.add,
            )

        def warm_up(count):
            unread = psum.tile([P, N_TILE], F32, name="acc", bufs=6)
            for i in range(count):
                nc.tensor.matmul(unread[:], lhsT=ones[:, :P], rhs=ones[:], start=(i == 0), stop=(i == count - 1))

        warm_up(6)
        transpose(0, split_words(0))
        transpose(1, split_words(1))
        warm_up(2)
        for first in range(0, 2 * PASSES, 2):
            quantize(first, first + 2)

        k_out = out_1.rearrange("b t h d -> t b (h d)")
        q_out = out_0.rearrange("b t h d -> t b (h d)")
        column_tiles = [(k_words, k_scale, 1, k_out)]
        for j in range(q_tiles):
            plane = (q_scale_lo, q_scale_hi)[j // 2]
            column_tiles.append(
                (q_words[j], plane[:, :, N_TILE * (j % 2) : N_TILE * (j % 2 + 1)], 0, q_out[:, :, N_TILE * j : N_TILE * (j + 1)])
            )
        jobs = [(b0, tile) for b0 in (0, 2) for tile in column_tiles]

        def inverse_rms(rstd, sums):
            nc.scalar.activation(out=rstd, in_=sums, func=ACT.Abs_reciprocal_sqrt, scale=1.0 / D, bias=RMS_EPS)

        def store(dest, result):
            nc.sync.dma_start(out=dest, in_=result.rearrange("p (b h) d -> p b (h d)", h=HEADS))

        def scale_and_store(result, rstd, dest):
            for h in range(HEADS):
                nc.scalar.activation(out=result[:, h, :], in_=result[:, h, :], func=ACT.Copy, scale=rstd[:, h : h + 1])
            store(dest[:, 0:1, :], result[:, lower, :])

        lower, upper = slice(0, HEADS), slice(HEADS, 2 * HEADS)
        last = len(jobs) - 1
        unscaled = {}
        closing = []
        for n, (b0, (w_tile, plane_cols, which, columns)) in enumerate(jobs):
            plain = n in PLAIN_PAIRS
            dest = columns[:, b0 : b0 + 2, :]
            prod = work.tile([P, 2, 2 * HEADS, D], F32, bufs=4)
            result = work.tile([P, 2 * HEADS, D], F32, bufs=6)
            sums = work.tile([P, 2 * HEADS], F32, bufs=6)
            rstd = work.tile([P, 2 * HEADS], F32, bufs=6)
            first = project(b0, w_tile, plane_cols, sums[:, lower])
            if n == 0:
                build_table(spread_gains())
            if not plain:
                inverse_rms(rstd[:, lower], sums[:, lower])
            if n == TRANSPOSE_AFTER:
                transpose(2, word_view(2))
            second = project(b0 + 1, w_tile, plane_cols, sums[:, upper])
            if plain:
                inverse_rms(rstd[:], sums[:])
            else:
                inverse_rms(rstd[:, upper], sums[:, upper])
            if n == TRANSPOSE_AFTER:
                transpose(3, word_view(3))
            if n - SCALE_LAG in unscaled:
                scale_and_store(*unscaled.pop(n - SCALE_LAG))
            if plain:
                plain_products(first, which, prod[:, :, lower, :])
            else:
                products(first, rstd[:, lower], which, prod[:, :, lower, :])
            products(second, rstd[:, upper], which, prod[:, :, upper, :])
            if n == TRANSPOSE_AFTER:
                quantize(2 * PASSES, 4 * PASSES)
            if n < last - 1:
                add_halves(nc.gpsimd, result[:], prod[:])
                if plain:
                    store(dest[:, 1:2, :], result[:, upper, :])
                    unscaled[n] = (result, rstd, dest)
                else:
                    store(dest, result[:])
            else:
                closing.append((result[:, lower, :], prod[:, :, lower, :], dest[:, 0:1, :]))
                closing.append((result[:, upper, :], prod[:, :, upper, :], dest[:, 1:2, :]))
        for waiting in unscaled.values():
            scale_and_store(*waiting)
        for i, (result, prod, dest) in enumerate(closing):
            add_halves(nc.gpsimd if i == 0 else nc.vector, result, prod)
            store(dest, result)
